import numpy as np
import ml_dtypes


def mxq(x, axis, fmt="e4m3"):
    dtype, down = {"e4m3": (ml_dtypes.float8_e4m3fn, 7), "e5m2": (ml_dtypes.float8_e5m2, 14)}[fmt]
    v = np.moveaxis(np.asarray(x, np.float32).astype(ml_dtypes.bfloat16).astype(np.float64), axis, -1)
    blocks = v.reshape(v.shape[:-1] + (-1, 32))
    amax = np.abs(blocks).max(-1, keepdims=True)
    byte = np.maximum(np.where(amax > 0, np.frexp(amax)[1] - 1 + 127, 0) - down, 1)
    scale = np.exp2(byte - 127.0)
    codes = (blocks / scale).astype(np.float32).astype(dtype).astype(np.float64)
    return np.moveaxis((codes * scale).reshape(v.shape), -1, axis)


WIDE = False


def mx_kscale(k):
    if not WIDE:
        return np.ones(k)
    levels = np.array([10, -10, 5, -5, 0])
    a = np.random.permutation(np.resize(levels, k // 512 * 4)).reshape(k // 512, 4)
    idx = np.arange(k)
    return np.exp2(a[idx // 512, idx % 128 // 32])


BF16 = ml_dtypes.bfloat16


def bf(x):
    return np.asarray(x, np.float32).astype(BF16)


def f64(x):
    return np.asarray(x).astype(np.float64)


N, D_IN, D_HID, D_OUT = 1024, 1025, 4097, 1025
K = D_IN - 1
M = D_HID - 1
EPS = 1e-7
MAX_TAN_NORM = 10.0


def arccosh(v):
    return np.log(v + np.sqrt(v * v - 1.0))


def cosh(v):
    return 0.5 * (np.exp(v) + np.exp(-v))


def sinh(v):
    return 0.5 * (np.exp(v) - np.exp(-v))


def setup_inputs():
    s = mx_kscale(K)
    c = np.sqrt(np.mean(s * s))
    g = np.random.standard_normal((N, K)) * s
    r = np.random.uniform(2.0, 4.0, (N, 1))
    xs = sinh(r) * g / np.sqrt(np.sum(g * g, axis=1, keepdims=True))
    col = np.concatenate([np.ones(1), c / s])
    return {"x_hyp": bf(np.concatenate([cosh(r), xs], axis=1)),
            "W": bf(np.random.standard_normal((D_HID, D_IN)) * 2.8 / np.sqrt(M) * col[None, :]),
            "b": bf(np.random.standard_normal(D_HID) * 3.0 / np.sqrt(M))}


def reference(x_hyp, W, b):
    x = f64(x_hyp)
    x0, xs = x[:, :1], x[:, 1:]
    d = arccosh(np.maximum(x0, 1.0 + EPS))
    ns = np.maximum(np.sqrt(np.sum(xs * xs, axis=1, keepdims=True)), EPS)
    ts = d * xs / ns
    us = (mxq(ts, 1, "e4m3") @ mxq(f64(W)[1:, 1:], 1, "e4m3").T) + f64(b)[1:]
    n = np.maximum(np.sqrt(np.sum(us * us, axis=1, keepdims=True)), EPS)
    nc = np.minimum(n, MAX_TAN_NORM)
    usc = us * (nc / n)
    return np.concatenate([cosh(nc), sinh(nc) * usc / nc], axis=1)

@@ -1,0 +1,386 @@
+from contextlib import ExitStack
+
+import concourse.mybir as mybir
+from concourse.masks import make_identity
+
+FLOPS = 2 * 1024 * 4096 * 1024
+
+F32 = mybir.dt.float32
+BF16 = mybir.dt.bfloat16
+U32 = mybir.dt.uint32
+U8 = mybir.dt.uint8
+FP8X4 = mybir.dt.float8_e4m3fn_x4
+ALU = mybir.AluOpType
+ACT = mybir.ActivationFunctionType
+AX = mybir.AxisListType
+
+P = 128
+NT = 8
+NCH = 8
+PAD = 32
+XP = PAD + 1024
+WP = XP // 2
+OPAD = 8
+WBUFS = 4
+X_LAG = 2
+I_SPLIT = (768, 1280, 1024, 1024)
+
+
+def tile_lorentzmlp_pa_kernel(tc, x_hyp, W, b, out):
+    nc = tc.nc
+    with ExitStack() as ctx:
+        ctx.enter_context(tc.manual_schedule())
+        const = ctx.enter_context(tc.tile_pool(name="const", bufs=1))
+        wpool = ctx.enter_context(tc.tile_pool(name="wraw", bufs=WBUFS))
+        gpool = ctx.enter_context(tc.tile_pool(name="grouped", bufs=2))
+        tpool = ctx.enter_context(tc.tile_pool(name="ts", bufs=4))
+        spool = ctx.enter_context(tc.tile_pool(name="scratch", bufs=2))
+        opool = ctx.enter_context(tc.tile_pool(name="outs", bufs=4))
+        small = ctx.enter_context(tc.tile_pool(name="small", bufs=3))
+        psum = ctx.enter_context(tc.psum_pool(name="psum", bufs=8))
+
+        xraw = const.tile([P, NT * XP], BF16, align_bytes=64)
+        xr3 = xraw[:].rearrange("p (m c) -> p m c", c=XP)
+        xsrc = x_hyp.rearrange("(m p) c -> p m c", p=P)
+        wsrc = W[1:4097, :].rearrange("(c t p) k -> c p t k", t=4, p=P)
+        xq = const.tile([P, NT * 256], U32, align_bytes=64)
+        xsc = const.tile([P, NT * 256], U8, align_bytes=64)
+        wq = const.tile([P, NCH * 1024], U32, align_bytes=64)
+        wsc = const.tile([P, NCH * 1024], U8, align_bytes=64)
+        bias = const.tile([P, 4096], BF16)
+        ident_f = const.tile([P, P], F32)
+        ident_b = const.tile([P, P], BF16)
+        one = const.tile([P, 1], F32)
+        ex16 = const.tile([P, 16], F32)
+        ex2 = const.tile([P, 2], F32)
+        c14 = const.tile([P, 2], F32)
+        warm = const.tile([P, 2], F32)
+        pw = const.tile([P, 32], F32)
+        pw3 = pw[:].rearrange("p (a i) -> p a i", i=8)
+        v = const.tile([P, 8], F32)
+        v3 = v[:].rearrange("p (a i) -> p a i", a=2)
+        vp1 = const.tile([P, 8], F32)
+        po = const.tile([P, 16], F32)
+        po3 = po[:].rearrange("p (a i) -> p a i", i=4)
+        ex3 = ex16[:].rearrange("p (a i) -> p a i", i=4)
+        warg = const.tile([P, 8], F32)
+        dist = const.tile([P, 8], F32)
+        sx = const.tile([P, 8], F32)
+
+        wraw_t = {}
+        wbank = {}
+        wg_t = {}
+        ts_t = {}
+        xbank = {}
+        xg_t = {}
+
+        def load_w(c):
+            wraw = wpool.tile([P, 4 * XP], BF16, align_bytes=64, name="wraw")
+            nc.sync.dma_start(
+                out=wraw[:].rearrange("p (t k) -> p t k", k=XP)[:, :, PAD - 1 : XP],
+                in_=wsrc[c],
+            )
+            wraw_t[c] = wraw
+
+        def row_norm(m):
+            xs = xr3[:, m, PAD:XP]
+            if m % 2 == 0:
+                junk = spool.tile([P, 1024], BF16, name="junk")
+                nc.scalar.activation(
+                    out=junk[:], in_=xs, func=ACT.Square,
+                    accum_out=pw3[:, 0, m // 2 : m // 2 + 1],
+                )
+            else:
+                junkv = spool.tile([P, 1024], F32, name="junkv")
+                nc.vector.scalar_tensor_tensor(
+                    out=junkv[:], in0=xs, scalar=1.0, in1=xs,
+                    op0=ALU.mult, op1=ALU.mult,
+                    accum_out=pw3[:, 1, m // 2 : m // 2 + 1],
+                )
+
+        def scale_x(m):
+            j = 4 * (m % 2) + m // 2
+            ts = tpool.tile([P, 1024], BF16, align_bytes=64, name="ts")
+            nc.gpsimd.tensor_scalar(
+                out=ts[:].rearrange("p (e q) -> p e q", e=2),
+                in0=xr3[:, m, PAD:XP].rearrange("p (q e) -> p e q", e=2),
+                scalar1=sx[:, j : j + 1], scalar2=0.0, op0=ALU.mult, op1=ALU.add,
+            )
+            ts_t[m] = ts
+
+        def transpose_x(m):
+            xt = psum.tile([P, 1024], BF16, tag="bank", name="xt")
+            for g in range(2):
+                for u in range(2):
+                    for e in range(2):
+                        col = (g * 4 + 2 * u + e) * P
+                        src = e * 512 + 256 * g + 128 * u
+                        nc.tensor.transpose(
+                            xt[:, col : col + P], ts_t[m][:, src : src + P], ident_b[:]
+                        )
+            xbank[m] = xt
+
+        def regroup_x(m):
+            xg = gpool.tile([P, 1024], BF16, align_bytes=64, name="xg")
+            dst = xg[:].rearrange("p (g r t) -> p g r t", g=2, t=4)
+            src = xbank[m][:].rearrange("p (g t r) -> p g r t", g=2, t=4)
+            if m >= NT - X_LAG:
+                nc.scalar.copy(out=dst, in_=src)
+            else:
+                nc.vector.tensor_copy(out=dst, in_=src)
+            xg_t[m] = xg
+
+        def quantise_x(m):
+            nc.vector.quantize_mx(
+                out=xq[:, m * 256 : (m + 1) * 256].bitcast(FP8X4),
+                scales=xsc[:, m * 256 : (m + 1) * 256],
+                in_=xg_t[m][:],
+            )
+
+        def transpose_w(c):
+            wf = wraw_t[c][:].bitcast(F32)
+            for g in range(2):
+                for tp in range(2):
+                    wt = psum.tile([P, 512], F32, tag="bank", name="wt")
+                    for tl in range(2):
+                        for u in range(2):
+                            col = (tl * 2 + u) * P
+                            src = (2 * tp + tl) * WP + PAD // 2 + 256 * g + 128 * u
+                            nc.tensor.transpose(
+                                wt[:, col : col + P], wf[:, src : src + P], ident_f[:]
+                            )
+                    wbank[(c, 2 * g + tp)] = wt
+
+        def copy_w(c, k, on_vector):
+            if c not in wg_t:
+                wg = gpool.tile([P, 4096], BF16, align_bytes=64, name="wg")
+                wg_t[c] = wg
+            wgf = wg_t[c][:].bitcast(F32)
+            dst = wgf[:, k * 512 : (k + 1) * 512].rearrange(
+                "p (tl n u) -> p tl n u", tl=2, u=2
+            )
+            src = wbank[(c, k)][:].rearrange("p (tl u n) -> p tl n u", tl=2, u=2)
+            if on_vector:
+                nc.vector.tensor_copy(out=dst, in_=src)
+            else:
+                nc.scalar.copy(out=dst, in_=src)
+
+        def quantise_w(c):
+            nc.vector.quantize_mx(
+                out=wq[:, c * 1024 : (c + 1) * 1024].bitcast(FP8X4),
+                scales=wsc[:, c * 1024 : (c + 1) * 1024],
+                in_=wg_t[c][:],
+            )
+
+        for h in range(4):
+            nc.sync.dma_start(
+                out=xr3[:, 2 * h : 2 * h + 2, PAD - 1 : XP],
+                in_=xsrc[:, 2 * h : 2 * h + 2, :],
+            )
+        for c in range(WBUFS):
+            load_w(c)
+        make_identity(nc, ident_f[:])
+        make_identity(nc, ident_b[:])
+        nc.vector.memset(one[:], 1.0)
+        nc.vector.memset(ex16[:, 0:8], -0.5)
+        nc.vector.memset(ex16[:, 8:16], 0.5)
+        nc.vector.memset(ex2[:, 0:1], 0.5)
+        nc.vector.memset(ex2[:, 1:2], -0.5)
+        nc.vector.memset(c14[:, 0:1], 1.0)
+        nc.vector.memset(c14[:, 1:2], 4.0)
+        nc.scalar.activation(out=warm[:, 0:1], in_=one[:], func=ACT.Ln)
+        for m in range(NT - 1):
+            row_norm(m)
+        nc.vector.tensor_scalar_max(
+            out=v3, in0=xr3[:, :, PAD - 1].rearrange("p (i a) -> p a i", a=2),
+            scalar1=1.0 + 1e-7,
+        )
+        nc.vector.tensor_scalar_add(out=vp1[:], in0=v[:], scalar1=1.0)
+        nc.vector.scalar_tensor_tensor(
+            out=pw3[:, 2:4, 0:4], in0=v3, scalar=-1.0,
+            in1=vp1[:].rearrange("p (a i) -> p a i", a=2),
+            op0=ALU.add, op1=ALU.mult,
+        )
+        row_norm(NT - 1)
+        nc.gpsimd.tensor_tensor(
+            out=po3[:, 2:4, :], in0=pw3[:, 2:4, 0:4], in1=ex3[:, 2:4, :], op=ALU.pow
+        )
+        nc.gpsimd.tensor_tensor(
+            out=po3[:, 0:2, :], in0=pw3[:, 0:2, 0:4], in1=ex3[:, 0:2, :], op=ALU.pow
+        )
+        nc.vector.tensor_tensor(out=warg[:], in0=v[:], in1=po[:, 8:16], op=ALU.add)
+        nc.scalar.activation(out=dist[:], in_=warg[:], func=ACT.Ln)
+
+        for c in range(NCH + X_LAG):
+            if c < NCH:
+                transpose_w(c)
+            if 1 <= c <= NT:
+                transpose_x(c - 1)
+            if c + WBUFS < NCH:
+                load_w(c + WBUFS)
+            if c == NCH - 1:
+                for h in range(2):
+                    nc.sync.dma_start(
+                        out=bias[:, 2048 * h : 2048 * (h + 1)],
+                        in_=b[1 + 2048 * h : 1 + 2048 * (h + 1)].partition_broadcast(P),
+                    )
+            if c < NCH:
+                shared = c in (0, NCH - 1)
+                for k in range(4):
+                    if shared and k % 2 == 1:
+                        copy_w(c, k, True)
+                for k in range(4):
+                    if not (shared and k % 2 == 1):
+                        copy_w(c, k, False)
+            if c == 0:
+                nc.vector.scalar_tensor_tensor(
+                    out=sx[:], in0=po[:, 0:8], scalar=1e7, in1=dist[:],
+                    op0=ALU.min, op1=ALU.mult,
+                )
+                scale_x(0)
+                scale_x(1)
+            if c + 2 < NT:
+                scale_x(c + 2)
+            m = c - X_LAG
+            on_scalar = m >= NT - X_LAG
+            if 0 <= m:
+                regroup_x(m)
+            if 1 <= c <= NCH:
+                quantise_w(c - 1)
+            if 0 <= m and not on_scalar:
+                quantise_x(m)
+            if 0 <= m - 1 and m - 1 >= NT - X_LAG:
+                quantise_x(m - 1)
+        quantise_x(NT - 1)
+        nc.scalar.activation(out=warm[:, 1:2], in_=one[:], func=ACT.Exp)
+
+        ot_t = {}
+        acc_t = {}
+        nr_t = {}
+        ncl_t = {}
+        ep_t = {}
+        em_t = {}
+        sc_t = {}
+
+        def piece(m, i):
+            lo = OPAD + sum(I_SPLIT[:i])
+            return ot_t[m][:, lo : lo + I_SPLIT[i]]
+
+        def scale_on_gpsimd(seg, m):
+            nc.gpsimd.tensor_scalar(
+                out=seg, in0=seg, scalar1=sc_t[m][:, 0:1], scalar2=0.0,
+                op0=ALU.mult, op1=ALU.add,
+            )
+
+        def scale_on_vector(seg, m):
+            nc.vector.tensor_scalar(
+                out=seg, in0=seg, scalar1=sc_t[m][:, 0:1], scalar2=None, op0=ALU.mult
+            )
+
+        def store(m, lo, hi):
+            nc.sync.dma_start(
+                out=out[m * P : (m + 1) * P, lo:hi],
+                in_=ot_t[m][:, OPAD - 1 + lo : OPAD - 1 + hi],
+            )
+
+        def norm_start(m):
+            n2 = small.tile([P, 1], F32, name="n2")
+            nc.vector.tensor_reduce(out=n2[:], in_=acc_t[m][:], axis=AX.X, op=ALU.add)
+            pr = small.tile([P, 2], F32, name="pr")
+            nc.vector.scalar_tensor_tensor(
+                out=pr[:], in0=n2[:].to_broadcast([P, 2]), scalar=1e-14, in1=c14[:],
+                op0=ALU.max, op1=ALU.mult,
+            )
+            nr = small.tile([P, 2], F32, name="nr")
+            nc.gpsimd.tensor_tensor(out=nr[:], in0=pr[:], in1=ex2[:], op=ALU.pow)
+            ncl = small.tile([P, 1], F32, name="ncl")
+            nc.gpsimd.tensor_scalar(
+                out=ncl[:], in0=nr[:, 0:1], scalar1=10.0, scalar2=None, op0=ALU.min
+            )
+            nr_t[m] = nr
+            ncl_t[m] = ncl
+
+        def norm_exp(m):
+            ep = small.tile([P, 1], F32, name="ep")
+            nc.scalar.activation(out=ep[:], in_=ncl_t[m][:], func=ACT.Exp)
+            em = small.tile([P, 1], F32, name="em")
+            nc.scalar.activation(out=em[:], in_=ncl_t[m][:], func=ACT.Exp, scale=-1.0)
+            ep_t[m] = ep
+            em_t[m] = em
+
+        def norm_end(m):
+            sc = small.tile([P, 1], F32, name="sc")
+            nc.vector.tensor_scalar(
+                out=sc[:], in0=ep_t[m][:], scalar1=em_t[m][:, 0:1],
+                scalar2=nr_t[m][:, 1:2], op0=ALU.subtract, op1=ALU.mult,
+            )
+            nc.vector.tensor_scalar(
+                out=ot_t[m][:, OPAD - 1 : OPAD], in0=ep_t[m][:],
+                scalar1=em_t[m][:, 0:1], scalar2=0.5, op0=ALU.add, op1=ALU.mult,
+            )
+            sc_t[m] = sc
+
+        for m in range(NT):
+            last = m == NT - 1
+            hw = 1 if last else 2
+            ot = opool.tile([P, OPAD + 4096], F32, name="ot")
+            ot_t[m] = ot
+            acc = small.tile([P, NCH // hw], F32, name="acc8" if last else "acc")
+            acc_t[m] = acc
+            for c in range(NCH):
+                ps = psum.tile([P, 512], F32, tag="bank", name="ps")
+                for g in range(2):
+                    lo = (2 * m + g) * P
+                    ro = c * 1024 + g * 512
+                    nc.tensor.matmul_mx(
+                        out=ps[:],
+                        lhsT=xq[:, lo : lo + P].bitcast(FP8X4),
+                        lhsT_scale=xsc[:, lo : lo + P],
+                        rhs=wq[:, ro : ro + 512].bitcast(FP8X4),
+                        rhs_scale=wsc[:, ro : ro + 512],
+                        start=(g == 0),
+                        stop=(g == 1),
+                    )
+                nc.vector.tensor_tensor(
+                    out=ot[:, OPAD + 512 * c : OPAD + 512 * (c + 1)], in0=ps[:],
+                    in1=bias[:, 512 * c : 512 * (c + 1)], op=ALU.add,
+                )
+                if (c + 1) % hw == 0:
+                    h = c // hw
+                    junk = spool.tile([P, 1024], BF16, name="junk")
+                    nc.scalar.activation(
+                        out=junk[:, 0 : 512 * hw],
+                        in_=ot[:, OPAD + 512 * hw * h : OPAD + 512 * hw * (h + 1)],
+                        func=ACT.Square, accum_out=acc[:, h : h + 1],
+                    )
+                if m > 0 and c == 3:
+                    norm_start(m - 1)
+                    if m > 1:
+                        scale_on_gpsimd(piece(m - 2, 3), m - 2)
+                        store(m - 2, 2049, 4097)
+                if m > 0 and c == 4:
+                    norm_exp(m - 1)
+                if m > 0 and c == 6:
+                    norm_end(m - 1)
+                    scale_on_vector(piece(m - 1, 0), m - 1)
+                    scale_on_gpsimd(piece(m - 1, 1), m - 1)
+                    store(m - 1, 0, 2049)
+                    scale_on_gpsimd(piece(m - 1, 2), m - 1)
+
+        m = NT - 1
+        scale_on_vector(piece(m - 1, 3), m - 1)
+        store(m - 1, 2049, 4097)
+        norm_start(m)
+        norm_exp(m)
+        norm_end(m)
+        quarter = [ot_t[m][:, OPAD + 1024 * i : OPAD + 1024 * (i + 1)] for i in range(4)]
+        scale_on_vector(quarter[0], m)
+        store(m, 0, 1025)
+        scale_on_gpsimd(quarter[1], m)
+        store(m, 1025, 2049)
+        nc.scalar.activation(
+            out=quarter[2], in_=quarter[2], func=ACT.Copy, scale=sc_t[m][:, 0:1]
+        )
+        store(m, 2049, 3073)
+        scale_on_vector(quarter[3], m)
+        store(m, 3073, 4097)

@@ -37,7 +37,8 @@ def tile_lorentzmlp_pa_kernel(tc, x_hyp, W, b, out):
         spool = ctx.enter_context(tc.tile_pool(name="scratch", bufs=2))
         opool = ctx.enter_context(tc.tile_pool(name="outs", bufs=4))
         small = ctx.enter_context(tc.tile_pool(name="small", bufs=3))
-        psum = ctx.enter_context(tc.psum_pool(name="psum", bufs=8))
+        psum = ctx.enter_context(tc.psum_pool(name="psum", bufs=7))
+        hpool = ctx.enter_context(tc.psum_pool(name="heat", bufs=1))
 
         xraw = const.tile([P, NT * XP], BF16, align_bytes=64)
         xr3 = xraw[:].rearrange("p (m c) -> p m c", c=XP)
@@ -66,6 +67,16 @@ def tile_lorentzmlp_pa_kernel(tc, x_hyp, W, b, out):
         warg = const.tile([P, 8], F32)
         dist = const.tile([P, 8], F32)
         sx = const.tile([P, 8], F32)
+
+        heat = hpool.tile([P, 512], F32)
+
+        def keep_clock(n):
+            lo = (NT - 1) * XP + PAD
+            for i in range(n):
+                nc.tensor.matmul(
+                    out=heat[:], lhsT=ident_b[:], rhs=xraw[:, lo : lo + 512],
+                    start=True, stop=True,
+                )
 
         wraw_t = {}
         wbank = {}
@@ -150,6 +161,8 @@ def tile_lorentzmlp_pa_kernel(tc, x_hyp, W, b, out):
                                 wt[:, col : col + P], wf[:, src : src + P], ident_f[:]
                             )
                     wbank[(c, 2 * g + tp)] = wt
+                    if tp == 1:
+                        keep_clock(1)
 
         def copy_w(c, k, on_vector):
             if c not in wg_t:
@@ -210,6 +223,8 @@ def tile_lorentzmlp_pa_kernel(tc, x_hyp, W, b, out):
         )
         nc.vector.tensor_tensor(out=warg[:], in0=v[:], in1=po[:, 8:16], op=ALU.add)
         nc.scalar.activation(out=dist[:], in_=warg[:], func=ACT.Ln)
+
+        keep_clock(8)
 
         for c in range(NCH + X_LAG):
             if c < NCH:

@@ -17,9 +17,9 @@ AX = mybir.AxisListType
 P = 128
 NT = 8
 NCH = 8
-PAD = 32
-XP = PAD + 1024
+XP = 1024
 WP = XP // 2
+HEAD = 16
 OPAD = 8
 WBUFS = 4
 X_LAG = 2
@@ -37,13 +37,14 @@ def tile_lorentzmlp_pa_kernel(tc, x_hyp, W, b, out):
         spool = ctx.enter_context(tc.tile_pool(name="scratch", bufs=2))
         opool = ctx.enter_context(tc.tile_pool(name="outs", bufs=4))
         small = ctx.enter_context(tc.tile_pool(name="small", bufs=3))
-        psum = ctx.enter_context(tc.psum_pool(name="psum", bufs=7))
-        hpool = ctx.enter_context(tc.psum_pool(name="heat", bufs=1))
+        psum = ctx.enter_context(tc.psum_pool(name="psum", bufs=8))
 
         xraw = const.tile([P, NT * XP], BF16, align_bytes=64)
         xr3 = xraw[:].rearrange("p (m c) -> p m c", c=XP)
         xsrc = x_hyp.rearrange("(m p) c -> p m c", p=P)
-        wsrc = W[1:4097, :].rearrange("(c t p) k -> c p t k", t=4, p=P)
+        wsrc = W[1:4097, 1:1025].rearrange("(c t p) k -> c p t k", t=4, p=P)
+        xhead = const.tile([P, NT * HEAD], BF16)
+        xh3 = xhead[:].rearrange("p (m s) -> p m s", s=HEAD)
         xq = const.tile([P, NT * 256], U32, align_bytes=64)
         xsc = const.tile([P, NT * 256], U8, align_bytes=64)
         wq = const.tile([P, NCH * 1024], U32, align_bytes=64)
@@ -68,16 +69,6 @@ def tile_lorentzmlp_pa_kernel(tc, x_hyp, W, b, out):
         dist = const.tile([P, 8], F32)
         sx = const.tile([P, 8], F32)
 
-        heat = hpool.tile([P, 512], F32)
-
-        def keep_clock(n):
-            lo = (NT - 1) * XP + PAD
-            for i in range(n):
-                nc.tensor.matmul(
-                    out=heat[:], lhsT=ident_b[:], rhs=xraw[:, lo : lo + 512],
-                    start=True, stop=True,
-                )
-
         wraw_t = {}
         wbank = {}
         wg_t = {}
@@ -88,13 +79,13 @@ def tile_lorentzmlp_pa_kernel(tc, x_hyp, W, b, out):
         def load_w(c):
             wraw = wpool.tile([P, 4 * XP], BF16, align_bytes=64, name="wraw")
             nc.sync.dma_start(
-                out=wraw[:].rearrange("p (t k) -> p t k", k=XP)[:, :, PAD - 1 : XP],
+                out=wraw[:].rearrange("p (t k) -> p t k", k=XP),
                 in_=wsrc[c],
             )
             wraw_t[c] = wraw
 
         def row_norm(m):
-            xs = xr3[:, m, PAD:XP]
+            xs = xr3[:, m, :]
             if m % 2 == 0:
                 junk = spool.tile([P, 1024], BF16, name="junk")
                 nc.scalar.activation(
@@ -114,7 +105,7 @@ def tile_lorentzmlp_pa_kernel(tc, x_hyp, W, b, out):
             ts = tpool.tile([P, 1024], BF16, align_bytes=64, name="ts")
             nc.gpsimd.tensor_scalar(
                 out=ts[:].rearrange("p (e q) -> p e q", e=2),
-                in0=xr3[:, m, PAD:XP].rearrange("p (q e) -> p e q", e=2),
+                in0=xr3[:, m, :].rearrange("p (q e) -> p e q", e=2),
                 scalar1=sx[:, j : j + 1], scalar2=0.0, op0=ALU.mult, op1=ALU.add,
             )
             ts_t[m] = ts
@@ -156,13 +147,11 @@ def tile_lorentzmlp_pa_kernel(tc, x_hyp, W, b, out):
                     for tl in range(2):
                         for u in range(2):
                             col = (tl * 2 + u) * P
-                            src = (2 * tp + tl) * WP + PAD // 2 + 256 * g + 128 * u
+                            src = (2 * tp + tl) * WP + 256 * g + 128 * u
                             nc.tensor.transpose(
                                 wt[:, col : col + P], wf[:, src : src + P], ident_f[:]
                             )
                     wbank[(c, 2 * g + tp)] = wt
-                    if tp == 1:
-                        keep_clock(1)
 
         def copy_w(c, k, on_vector):
             if c not in wg_t:
@@ -185,10 +174,11 @@ def tile_lorentzmlp_pa_kernel(tc, x_hyp, W, b, out):
                 in_=wg_t[c][:],
             )
 
+        nc.sync.dma_start(out=xh3, in_=xsrc[:, :, 0:HEAD])
         for h in range(4):
             nc.sync.dma_start(
-                out=xr3[:, 2 * h : 2 * h + 2, PAD - 1 : XP],
-                in_=xsrc[:, 2 * h : 2 * h + 2, :],
+                out=xr3[:, 2 * h : 2 * h + 2, :],
+                in_=xsrc[:, 2 * h : 2 * h + 2, 1:1025],
             )
         for c in range(WBUFS):
             load_w(c)
@@ -205,7 +195,7 @@ def tile_lorentzmlp_pa_kernel(tc, x_hyp, W, b, out):
         for m in range(NT - 1):
             row_norm(m)
         nc.vector.tensor_scalar_max(
-            out=v3, in0=xr3[:, :, PAD - 1].rearrange("p (i a) -> p a i", a=2),
+            out=v3, in0=xh3[:, :, 0].rearrange("p (i a) -> p a i", a=2),
             scalar1=1.0 + 1e-7,
         )
         nc.vector.tensor_scalar_add(out=vp1[:], in0=v[:], scalar1=1.0)
@@ -223,8 +213,6 @@ def tile_lorentzmlp_pa_kernel(tc, x_hyp, W, b, out):
         )
         nc.vector.tensor_tensor(out=warg[:], in0=v[:], in1=po[:, 8:16], op=ALU.add)
         nc.scalar.activation(out=dist[:], in_=warg[:], func=ACT.Ln)
-
-        keep_clock(8)
 
         for c in range(NCH + X_LAG):
             if c < NCH:

@@ -17,13 +17,12 @@ AX = mybir.AxisListType
 P = 128
 NT = 8
 NCH = 8
-XP = 1024
+PAD = 32
+XP = PAD + 1024
 WP = XP // 2
-HEAD = 16
 OPAD = 8
 WBUFS = 4
 X_LAG = 2
-I_SPLIT = (768, 1280, 1024, 1024)
 
 
 def tile_lorentzmlp_pa_kernel(tc, x_hyp, W, b, out):
@@ -42,9 +41,7 @@ def tile_lorentzmlp_pa_kernel(tc, x_hyp, W, b, out):
         xraw = const.tile([P, NT * XP], BF16, align_bytes=64)
         xr3 = xraw[:].rearrange("p (m c) -> p m c", c=XP)
         xsrc = x_hyp.rearrange("(m p) c -> p m c", p=P)
-        wsrc = W[1:4097, 1:1025].rearrange("(c t p) k -> c p t k", t=4, p=P)
-        xhead = const.tile([P, NT * HEAD], BF16)
-        xh3 = xhead[:].rearrange("p (m s) -> p m s", s=HEAD)
+        wsrc = W[1:4097, :].rearrange("(c t p) k -> c p t k", t=4, p=P)
         xq = const.tile([P, NT * 256], U32, align_bytes=64)
         xsc = const.tile([P, NT * 256], U8, align_bytes=64)
         wq = const.tile([P, NCH * 1024], U32, align_bytes=64)
@@ -53,18 +50,16 @@ def tile_lorentzmlp_pa_kernel(tc, x_hyp, W, b, out):
         ident_f = const.tile([P, P], F32)
         ident_b = const.tile([P, P], BF16)
         one = const.tile([P, 1], F32)
-        ex16 = const.tile([P, 16], F32)
         ex2 = const.tile([P, 2], F32)
-        c14 = const.tile([P, 2], F32)
         warm = const.tile([P, 2], F32)
-        pw = const.tile([P, 32], F32)
+        pw = const.tile([P, 16], F32)
         pw3 = pw[:].rearrange("p (a i) -> p a i", i=8)
+        pc = const.tile([P, 16], F32)
         v = const.tile([P, 8], F32)
         v3 = v[:].rearrange("p (a i) -> p a i", a=2)
         vp1 = const.tile([P, 8], F32)
         po = const.tile([P, 16], F32)
-        po3 = po[:].rearrange("p (a i) -> p a i", i=4)
-        ex3 = ex16[:].rearrange("p (a i) -> p a i", i=4)
+        rns = const.tile([P, 8], F32)
         warg = const.tile([P, 8], F32)
         dist = const.tile([P, 8], F32)
         sx = const.tile([P, 8], F32)
@@ -79,13 +74,13 @@ def tile_lorentzmlp_pa_kernel(tc, x_hyp, W, b, out):
         def load_w(c):
             wraw = wpool.tile([P, 4 * XP], BF16, align_bytes=64, name="wraw")
             nc.sync.dma_start(
-                out=wraw[:].rearrange("p (t k) -> p t k", k=XP),
+                out=wraw[:].rearrange("p (t k) -> p t k", k=XP)[:, :, PAD - 1 : XP],
                 in_=wsrc[c],
             )
             wraw_t[c] = wraw
 
         def row_norm(m):
-            xs = xr3[:, m, :]
+            xs = xr3[:, m, PAD:XP]
             if m % 2 == 0:
                 junk = spool.tile([P, 1024], BF16, name="junk")
                 nc.scalar.activation(
@@ -103,22 +98,22 @@ def tile_lorentzmlp_pa_kernel(tc, x_hyp, W, b, out):
         def scale_x(m):
             j = 4 * (m % 2) + m // 2
             ts = tpool.tile([P, 1024], BF16, align_bytes=64, name="ts")
-            nc.gpsimd.tensor_scalar(
-                out=ts[:].rearrange("p (e q) -> p e q", e=2),
-                in0=xr3[:, m, :].rearrange("p (q e) -> p e q", e=2),
-                scalar1=sx[:, j : j + 1], scalar2=0.0, op0=ALU.mult, op1=ALU.add,
+            nc.vector.tensor_scalar(
+                out=ts[:], in0=xr3[:, m, PAD:XP], scalar1=sx[:, j : j + 1],
+                scalar2=None, op0=ALU.mult,
             )
             ts_t[m] = ts
 
         def transpose_x(m):
             xt = psum.tile([P, 1024], BF16, tag="bank", name="xt")
+            ts3 = ts_t[m][:].rearrange("p (q e) -> p e q", e=2)
             for g in range(2):
                 for u in range(2):
                     for e in range(2):
                         col = (g * 4 + 2 * u + e) * P
-                        src = e * 512 + 256 * g + 128 * u
+                        src = 256 * g + 128 * u
                         nc.tensor.transpose(
-                            xt[:, col : col + P], ts_t[m][:, src : src + P], ident_b[:]
+                            xt[:, col : col + P], ts3[:, e, src : src + P], ident_b[:]
                         )
             xbank[m] = xt
 
@@ -126,7 +121,7 @@ def tile_lorentzmlp_pa_kernel(tc, x_hyp, W, b, out):
             xg = gpool.tile([P, 1024], BF16, align_bytes=64, name="xg")
             dst = xg[:].rearrange("p (g r t) -> p g r t", g=2, t=4)
             src = xbank[m][:].rearrange("p (g t r) -> p g r t", g=2, t=4)
-            if m >= NT - X_LAG:
+            if m % 2 == 1:
                 nc.scalar.copy(out=dst, in_=src)
             else:
                 nc.vector.tensor_copy(out=dst, in_=src)
@@ -147,7 +142,7 @@ def tile_lorentzmlp_pa_kernel(tc, x_hyp, W, b, out):
                     for tl in range(2):
                         for u in range(2):
                             col = (tl * 2 + u) * P
-                            src = (2 * tp + tl) * WP + 256 * g + 128 * u
+                            src = (2 * tp + tl) * WP + PAD // 2 + 256 * g + 128 * u
                             nc.tensor.transpose(
                                 wt[:, col : col + P], wf[:, src : src + P], ident_f[:]
                             )
@@ -174,45 +169,40 @@ def tile_lorentzmlp_pa_kernel(tc, x_hyp, W, b, out):
                 in_=wg_t[c][:],
             )
 
-        nc.sync.dma_start(out=xh3, in_=xsrc[:, :, 0:HEAD])
         for h in range(4):
             nc.sync.dma_start(
-                out=xr3[:, 2 * h : 2 * h + 2, :],
-                in_=xsrc[:, 2 * h : 2 * h + 2, 1:1025],
+                out=xr3[:, 2 * h : 2 * h + 2, PAD - 1 : XP],
+                in_=xsrc[:, 2 * h : 2 * h + 2, :],
             )
         for c in range(WBUFS):
             load_w(c)
         make_identity(nc, ident_f[:])
         make_identity(nc, ident_b[:])
         nc.vector.memset(one[:], 1.0)
-        nc.vector.memset(ex16[:, 0:8], -0.5)
-        nc.vector.memset(ex16[:, 8:16], 0.5)
         nc.vector.memset(ex2[:, 0:1], 0.5)
         nc.vector.memset(ex2[:, 1:2], -0.5)
-        nc.vector.memset(c14[:, 0:1], 1.0)
-        nc.vector.memset(c14[:, 1:2], 4.0)
-        nc.scalar.activation(out=warm[:, 0:1], in_=one[:], func=ACT.Ln)
+        nc.scalar.activation(out=warm[:, 0:1], in_=one[:], func=ACT.Sqrt)
         for m in range(NT - 1):
             row_norm(m)
         nc.vector.tensor_scalar_max(
-            out=v3, in0=xh3[:, :, 0].rearrange("p (i a) -> p a i", a=2),
+            out=v3, in0=xr3[:, :, PAD - 1].rearrange("p (i a) -> p a i", a=2),
             scalar1=1.0 + 1e-7,
         )
         nc.vector.tensor_scalar_add(out=vp1[:], in0=v[:], scalar1=1.0)
         nc.vector.scalar_tensor_tensor(
-            out=pw3[:, 2:4, 0:4], in0=v3, scalar=-1.0,
-            in1=vp1[:].rearrange("p (a i) -> p a i", a=2),
+            out=pc[:, 8:16], in0=v[:], scalar=-1.0, in1=vp1[:],
             op0=ALU.add, op1=ALU.mult,
         )
         row_norm(NT - 1)
-        nc.gpsimd.tensor_tensor(
-            out=po3[:, 2:4, :], in0=pw3[:, 2:4, 0:4], in1=ex3[:, 2:4, :], op=ALU.pow
+        nc.vector.tensor_scalar_max(
+            out=pc[:, 0:8].rearrange("p (a i) -> p a i", a=2), in0=pw3[:, :, 0:4],
+            scalar1=1e-14,
         )
-        nc.gpsimd.tensor_tensor(
-            out=po3[:, 0:2, :], in0=pw3[:, 0:2, 0:4], in1=ex3[:, 0:2, :], op=ALU.pow
-        )
+        nc.scalar.activation(out=po[:], in_=pc[:], func=ACT.Sqrt)
         nc.vector.tensor_tensor(out=warg[:], in0=v[:], in1=po[:, 8:16], op=ALU.add)
+        nc.vector.reciprocal(out=rns[:], in_=po[:, 0:8])
         nc.scalar.activation(out=dist[:], in_=warg[:], func=ACT.Ln)
+        nc.vector.tensor_tensor(out=sx[:], in0=rns[:], in1=dist[:], op=ALU.mult)
 
         for c in range(NCH + X_LAG):
             if c < NCH:
@@ -227,58 +217,55 @@ def tile_lorentzmlp_pa_kernel(tc, x_hyp, W, b, out):
                         out=bias[:, 2048 * h : 2048 * (h + 1)],
                         in_=b[1 + 2048 * h : 1 + 2048 * (h + 1)].partition_broadcast(P),
                     )
-            if c < NCH:
-                shared = c in (0, NCH - 1)
-                for k in range(4):
-                    if shared and k % 2 == 1:
-                        copy_w(c, k, True)
-                for k in range(4):
-                    if not (shared and k % 2 == 1):
-                        copy_w(c, k, False)
             if c == 0:
-                nc.vector.scalar_tensor_tensor(
-                    out=sx[:], in0=po[:, 0:8], scalar=1e7, in1=dist[:],
-                    op0=ALU.min, op1=ALU.mult,
-                )
                 scale_x(0)
                 scale_x(1)
-            if c + 2 < NT:
-                scale_x(c + 2)
+            if c < NCH:
+                for k in range(4):
+                    copy_w(c, k, False)
             m = c - X_LAG
-            on_scalar = m >= NT - X_LAG
+            if c == NCH:
+                quantise_w(c - 1)
             if 0 <= m:
                 regroup_x(m)
-            if 1 <= c <= NCH:
+            if 1 <= c < NCH:
                 quantise_w(c - 1)
-            if 0 <= m and not on_scalar:
+            if c + 2 < NT:
+                scale_x(c + 2)
+            if 0 <= m and m % 2 == 0:
                 quantise_x(m)
-            if 0 <= m - 1 and m - 1 >= NT - X_LAG:
+            if 0 <= m - 1 and m % 2 == 0:
                 quantise_x(m - 1)
-        quantise_x(NT - 1)
         nc.scalar.activation(out=warm[:, 1:2], in_=one[:], func=ACT.Exp)
 
         ot_t = {}
         acc_t = {}
+        n2_t = {}
         nr_t = {}
         ncl_t = {}
         ep_t = {}
         em_t = {}
         sc_t = {}
 
-        def piece(m, i):
-            lo = OPAD + sum(I_SPLIT[:i])
-            return ot_t[m][:, lo : lo + I_SPLIT[i]]
+        def columns(m, lo, hi):
+            return ot_t[m][:, OPAD + lo : OPAD + hi]
 
-        def scale_on_gpsimd(seg, m):
+        def scale_on_gpsimd(m, lo, hi):
+            seg = columns(m, lo, hi)
             nc.gpsimd.tensor_scalar(
                 out=seg, in0=seg, scalar1=sc_t[m][:, 0:1], scalar2=0.0,
                 op0=ALU.mult, op1=ALU.add,
             )
 
-        def scale_on_vector(seg, m):
+        def scale_on_vector(m, lo, hi):
+            seg = columns(m, lo, hi)
             nc.vector.tensor_scalar(
                 out=seg, in0=seg, scalar1=sc_t[m][:, 0:1], scalar2=None, op0=ALU.mult
             )
+
+        def scale_on_scalar(m, lo, hi):
+            seg = columns(m, lo, hi)
+            nc.scalar.activation(out=seg, in_=seg, func=ACT.Copy, scale=sc_t[m][:, 0:1])
 
         def store(m, lo, hi):
             nc.sync.dma_start(
@@ -286,13 +273,20 @@ def tile_lorentzmlp_pa_kernel(tc, x_hyp, W, b, out):
                 in_=ot_t[m][:, OPAD - 1 + lo : OPAD - 1 + hi],
             )
 
-        def norm_start(m):
+        def norm_sum(m):
             n2 = small.tile([P, 1], F32, name="n2")
-            nc.vector.tensor_reduce(out=n2[:], in_=acc_t[m][:], axis=AX.X, op=ALU.add)
+            junk8 = small.tile([P, 8], F32, name="junk8")
+            width = acc_t[m][:].shape[1]
+            nc.scalar.activation(
+                out=junk8[:, 0:width], in_=acc_t[m][:], func=ACT.Copy, accum_out=n2[:]
+            )
+            n2_t[m] = n2
+
+        def norm_root(m):
             pr = small.tile([P, 2], F32, name="pr")
-            nc.vector.scalar_tensor_tensor(
-                out=pr[:], in0=n2[:].to_broadcast([P, 2]), scalar=1e-14, in1=c14[:],
-                op0=ALU.max, op1=ALU.mult,
+            nc.gpsimd.tensor_scalar(
+                out=pr[:], in0=n2_t[m][:].to_broadcast([P, 2]), scalar1=1e-14,
+                scalar2=None, op0=ALU.max,
             )
             nr = small.tile([P, 2], F32, name="nr")
             nc.gpsimd.tensor_tensor(out=nr[:], in0=pr[:], in1=ex2[:], op=ALU.pow)
@@ -312,10 +306,14 @@ def tile_lorentzmlp_pa_kernel(tc, x_hyp, W, b, out):
             em_t[m] = em
 
         def norm_end(m):
+            sh = small.tile([P, 1], F32, name="sh")
+            nc.vector.tensor_scalar(
+                out=sh[:], in0=ep_t[m][:], scalar1=em_t[m][:, 0:1], scalar2=0.5,
+                op0=ALU.subtract, op1=ALU.mult,
+            )
             sc = small.tile([P, 1], F32, name="sc")
             nc.vector.tensor_scalar(
-                out=sc[:], in0=ep_t[m][:], scalar1=em_t[m][:, 0:1],
-                scalar2=nr_t[m][:, 1:2], op0=ALU.subtract, op1=ALU.mult,
+                out=sc[:], in0=sh[:], scalar1=nr_t[m][:, 1:2], scalar2=None, op0=ALU.mult
             )
             nc.vector.tensor_scalar(
                 out=ot_t[m][:, OPAD - 1 : OPAD], in0=ep_t[m][:],
@@ -356,34 +354,34 @@ def tile_lorentzmlp_pa_kernel(tc, x_hyp, W, b, out):
                         in_=ot[:, OPAD + 512 * hw * h : OPAD + 512 * hw * (h + 1)],
                         func=ACT.Square, accum_out=acc[:, h : h + 1],
                     )
-                if m > 0 and c == 3:
-                    norm_start(m - 1)
+                if m == 0 and c == 3:
+                    quantise_x(NT - 1)
+                if m > 0 and c == 1:
+                    norm_root(m - 1)
                     if m > 1:
-                        scale_on_gpsimd(piece(m - 2, 3), m - 2)
+                        scale_on_gpsimd(m - 2, 3072, 4096)
                         store(m - 2, 2049, 4097)
-                if m > 0 and c == 4:
+                if m > 0 and c == 3:
                     norm_exp(m - 1)
-                if m > 0 and c == 6:
-                    norm_end(m - 1)
-                    scale_on_vector(piece(m - 1, 0), m - 1)
-                    scale_on_gpsimd(piece(m - 1, 1), m - 1)
-                    store(m - 1, 0, 2049)
-                    scale_on_gpsimd(piece(m - 1, 2), m - 1)
+                if c == NCH - 1:
+                    norm_sum(m)
+                    if m > 0:
+                        norm_end(m - 1)
+                        scale_on_vector(m - 1, 0, 2048)
+                        store(m - 1, 0, 2049)
+                        scale_on_gpsimd(m - 1, 2048, 3072)
 
         m = NT - 1
-        scale_on_vector(piece(m - 1, 3), m - 1)
+        scale_on_vector(m - 1, 3072, 4096)
         store(m - 1, 2049, 4097)
-        norm_start(m)
+        norm_root(m)
         norm_exp(m)
         norm_end(m)
-        quarter = [ot_t[m][:, OPAD + 1024 * i : OPAD + 1024 * (i + 1)] for i in range(4)]
-        scale_on_vector(quarter[0], m)
+        scale_on_vector(m, 0, 1024)
         store(m, 0, 1025)
-        scale_on_gpsimd(quarter[1], m)
+        scale_on_gpsimd(m, 1024, 2048)
         store(m, 1025, 2049)
-        nc.scalar.activation(
-            out=quarter[2], in_=quarter[2], func=ACT.Copy, scale=sc_t[m][:, 0:1]
-        )
+        scale_on_scalar(m, 2048, 3072)
         store(m, 2049, 3073)
-        scale_on_vector(quarter[3], m)
+        scale_on_vector(m, 3072, 4096)
         store(m, 3073, 4097)

@@ -41,7 +41,7 @@ def tile_lorentzmlp_pa_kernel(tc, x_hyp, W, b, out):
         xraw = const.tile([P, NT * XP], BF16, align_bytes=64)
         xr3 = xraw[:].rearrange("p (m c) -> p m c", c=XP)
         xsrc = x_hyp.rearrange("(m p) c -> p m c", p=P)
-        wsrc = W[1:4097, :].rearrange("(c t p) k -> c p t k", t=4, p=P)
+        wsrc = W[1:4097, :].rearrange("(c t q e) k -> c e q t k", t=4, q=P // 2, e=2)
         xq = const.tile([P, NT * 256], U32, align_bytes=64)
         xsc = const.tile([P, NT * 256], U8, align_bytes=64)
         wq = const.tile([P, NCH * 1024], U32, align_bytes=64)
@@ -73,10 +73,9 @@ def tile_lorentzmlp_pa_kernel(tc, x_hyp, W, b, out):
 
         def load_w(c):
             wraw = wpool.tile([P, 4 * XP], BF16, align_bytes=64, name="wraw")
-            nc.sync.dma_start(
-                out=wraw[:].rearrange("p (t k) -> p t k", k=XP)[:, :, PAD - 1 : XP],
-                in_=wsrc[c],
-            )
+            wr3 = wraw[:].rearrange("p (t k) -> p t k", k=XP)
+            nc.sync.dma_start(out=wr3[0:P:2, :, PAD:XP], in_=wsrc[c, 0][:, :, 1:1025])
+            nc.sync.dma_start(out=wr3[1:P:2, :, PAD - 1 : XP], in_=wsrc[c, 1])
             wraw_t[c] = wraw
 
         def row_norm(m):

@@ -41,7 +41,7 @@ def tile_lorentzmlp_pa_kernel(tc, x_hyp, W, b, out):
         xraw = const.tile([P, NT * XP], BF16, align_bytes=64)
         xr3 = xraw[:].rearrange("p (m c) -> p m c", c=XP)
         xsrc = x_hyp.rearrange("(m p) c -> p m c", p=P)
-        wsrc = W[1:4097, :].rearrange("(c t q e) k -> c e q t k", t=4, q=P // 2, e=2)
+        wsrc = W[1:4097, :].rearrange("(c t p) k -> c p t k", t=4, p=P)
         xq = const.tile([P, NT * 256], U32, align_bytes=64)
         xsc = const.tile([P, NT * 256], U8, align_bytes=64)
         wq = const.tile([P, NCH * 1024], U32, align_bytes=64)
@@ -73,9 +73,10 @@ def tile_lorentzmlp_pa_kernel(tc, x_hyp, W, b, out):
 
         def load_w(c):
             wraw = wpool.tile([P, 4 * XP], BF16, align_bytes=64, name="wraw")
-            wr3 = wraw[:].rearrange("p (t k) -> p t k", k=XP)
-            nc.sync.dma_start(out=wr3[0:P:2, :, PAD:XP], in_=wsrc[c, 0][:, :, 1:1025])
-            nc.sync.dma_start(out=wr3[1:P:2, :, PAD - 1 : XP], in_=wsrc[c, 1])
+            nc.sync.dma_start(
+                out=wraw[:].rearrange("p (t k) -> p t k", k=XP)[:, :, PAD - 1 : XP],
+                in_=wsrc[c],
+            )
             wraw_t[c] = wraw
 
         def row_norm(m):
@@ -120,7 +121,7 @@ def tile_lorentzmlp_pa_kernel(tc, x_hyp, W, b, out):
             xg = gpool.tile([P, 1024], BF16, align_bytes=64, name="xg")
             dst = xg[:].rearrange("p (g r t) -> p g r t", g=2, t=4)
             src = xbank[m][:].rearrange("p (g t r) -> p g r t", g=2, t=4)
-            if m % 2 == 1:
+            if m % 2 == 1 and m >= NT // 2:
                 nc.scalar.copy(out=dst, in_=src)
             else:
                 nc.vector.tensor_copy(out=dst, in_=src)
@@ -231,9 +232,9 @@ def tile_lorentzmlp_pa_kernel(tc, x_hyp, W, b, out):
                 quantise_w(c - 1)
             if c + 2 < NT:
                 scale_x(c + 2)
-            if 0 <= m and m % 2 == 0:
+            if 0 <= m and not (m % 2 == 1 and m >= NT // 2):
                 quantise_x(m)
-            if 0 <= m - 1 and m % 2 == 0:
+            if m % 2 == 0 and m - 1 >= NT // 2:
                 quantise_x(m - 1)
         nc.scalar.activation(out=warm[:, 1:2], in_=one[:], func=ACT.Exp)
 
@@ -366,14 +367,19 @@ def tile_lorentzmlp_pa_kernel(tc, x_hyp, W, b, out):
                     norm_sum(m)
                     if m > 0:
                         norm_end(m - 1)
-                        scale_on_vector(m - 1, 0, 2048)
-                        store(m - 1, 0, 2049)
-                        scale_on_gpsimd(m - 1, 2048, 3072)
+                        scale_on_vector(m - 1, 0, 1536)
+                        if not last:
+                            scale_on_gpsimd(m - 1, 1536, 2048)
+                            store(m - 1, 0, 2049)
+                            scale_on_gpsimd(m - 1, 2048, 3072)
 
         m = NT - 1
+        norm_root(m)
+        scale_on_vector(m - 1, 1536, 2048)
+        store(m - 1, 0, 2049)
+        scale_on_scalar(m - 1, 2048, 3072)
         scale_on_vector(m - 1, 3072, 4096)
         store(m - 1, 2049, 4097)
-        norm_root(m)
         norm_exp(m)
         norm_end(m)
         scale_on_vector(m, 0, 1024)

@@ -360,7 +360,7 @@ def tile_lorentzmlp_pa_kernel(tc, x_hyp, W, b, out):
                     norm_root(m - 1)
                     if m > 1:
                         scale_on_gpsimd(m - 2, 3072, 4096)
-                        store(m - 2, 2049, 4097)
+                        store(m - 2, 0, 4097)
                 if m > 0 and c == 3:
                     norm_exp(m - 1)
                 if c == NCH - 1:
@@ -370,23 +370,18 @@ def tile_lorentzmlp_pa_kernel(tc, x_hyp, W, b, out):
                         scale_on_vector(m - 1, 0, 1536)
                         if not last:
                             scale_on_gpsimd(m - 1, 1536, 2048)
-                            store(m - 1, 0, 2049)
                             scale_on_gpsimd(m - 1, 2048, 3072)
 
         m = NT - 1
         norm_root(m)
         scale_on_vector(m - 1, 1536, 2048)
-        store(m - 1, 0, 2049)
         scale_on_scalar(m - 1, 2048, 3072)
         scale_on_vector(m - 1, 3072, 4096)
-        store(m - 1, 2049, 4097)
+        store(m - 1, 0, 4097)
         norm_exp(m)
         norm_end(m)
         scale_on_vector(m, 0, 1024)
-        store(m, 0, 1025)
         scale_on_gpsimd(m, 1024, 2048)
-        store(m, 1025, 2049)
         scale_on_scalar(m, 2048, 3072)
-        store(m, 2049, 3073)
         scale_on_vector(m, 3072, 4096)
-        store(m, 3073, 4097)
+        store(m, 0, 4097)

@@ -9,6 +9,7 @@ F32 = mybir.dt.float32
 BF16 = mybir.dt.bfloat16
 U32 = mybir.dt.uint32
 U8 = mybir.dt.uint8
+I32 = mybir.dt.int32
 FP8X4 = mybir.dt.float8_e4m3fn_x4
 ALU = mybir.AluOpType
 ACT = mybir.ActivationFunctionType
@@ -47,6 +48,8 @@ def tile_lorentzmlp_pa_kernel(tc, x_hyp, W, b, out):
         wq = const.tile([P, NCH * 1024], U32, align_bytes=64)
         wsc = const.tile([P, NCH * 1024], U8, align_bytes=64)
         bias = const.tile([P, 4096], BF16)
+        brow = const.tile([P, 4096], BF16)
+        ones = const.tile([P, P], BF16)
         ident_f = const.tile([P, P], F32)
         ident_b = const.tile([P, P], BF16)
         one = const.tile([P, 1], F32)
@@ -70,6 +73,7 @@ def tile_lorentzmlp_pa_kernel(tc, x_hyp, W, b, out):
         ts_t = {}
         xbank = {}
         xg_t = {}
+        bbank = {}
 
         def load_w(c):
             wraw = wpool.tile([P, 4 * XP], BF16, align_bytes=64, name="wraw")
@@ -162,6 +166,21 @@ def tile_lorentzmlp_pa_kernel(tc, x_hyp, W, b, out):
             else:
                 nc.scalar.copy(out=dst, in_=src)
 
+        def spread_bias(c):
+            bp = psum.tile([P, 512], F32, tag="bank", name="bp")
+            nc.tensor.matmul(
+                out=bp[:], lhsT=ones[:], rhs=brow[:, 512 * c : 512 * (c + 1)],
+                start=True, stop=True,
+            )
+            bbank[c] = bp
+
+        def copy_bias(c):
+            dst = bias[:, 512 * c : 512 * (c + 1)]
+            if c % 2 == 1:
+                nc.scalar.copy(out=dst, in_=bbank[c][:])
+            else:
+                nc.vector.tensor_copy(out=dst, in_=bbank[c][:])
+
         def quantise_w(c):
             nc.vector.quantize_mx(
                 out=wq[:, c * 1024 : (c + 1) * 1024].bitcast(FP8X4),
@@ -169,6 +188,9 @@ def tile_lorentzmlp_pa_kernel(tc, x_hyp, W, b, out):
                 in_=wg_t[c][:],
             )
 
+        nc.vector.memset(brow[:].bitcast(I32), 0)
+        nc.scalar.dma_start(out=brow[0:1, :], in_=b[1:4097].unsqueeze(0))
+        nc.vector.memset(ones[:], 1.0)
         for h in range(4):
             nc.sync.dma_start(
                 out=xr3[:, 2 * h : 2 * h + 2, PAD - 1 : XP],
@@ -211,18 +233,15 @@ def tile_lorentzmlp_pa_kernel(tc, x_hyp, W, b, out):
                 transpose_x(c - 1)
             if c + WBUFS < NCH:
                 load_w(c + WBUFS)
-            if c == NCH - 1:
-                for h in range(2):
-                    nc.sync.dma_start(
-                        out=bias[:, 2048 * h : 2048 * (h + 1)],
-                        in_=b[1 + 2048 * h : 1 + 2048 * (h + 1)].partition_broadcast(P),
-                    )
+            if c < NCH:
+                spread_bias(c)
             if c == 0:
                 scale_x(0)
                 scale_x(1)
             if c < NCH:
                 for k in range(4):
                     copy_w(c, k, False)
+                copy_bias(c)
             m = c - X_LAG
             if c == NCH:
                 quantise_w(c - 1)
@@ -360,7 +379,7 @@ def tile_lorentzmlp_pa_kernel(tc, x_hyp, W, b, out):
                     norm_root(m - 1)
                     if m > 1:
                         scale_on_gpsimd(m - 2, 3072, 4096)
-                        store(m - 2, 0, 4097)
+                        store(m - 2, 2049, 4097)
                 if m > 0 and c == 3:
                     norm_exp(m - 1)
                 if c == NCH - 1:
@@ -370,18 +389,23 @@ def tile_lorentzmlp_pa_kernel(tc, x_hyp, W, b, out):
                         scale_on_vector(m - 1, 0, 1536)
                         if not last:
                             scale_on_gpsimd(m - 1, 1536, 2048)
+                            store(m - 1, 0, 2049)
                             scale_on_gpsimd(m - 1, 2048, 3072)
 
         m = NT - 1
         norm_root(m)
         scale_on_vector(m - 1, 1536, 2048)
+        store(m - 1, 0, 2049)
         scale_on_scalar(m - 1, 2048, 3072)
         scale_on_vector(m - 1, 3072, 4096)
-        store(m - 1, 0, 4097)
+        store(m - 1, 2049, 4097)
         norm_exp(m)
         norm_end(m)
         scale_on_vector(m, 0, 1024)
+        store(m, 0, 1025)
         scale_on_gpsimd(m, 1024, 2048)
+        store(m, 1025, 2049)
         scale_on_scalar(m, 2048, 3072)
+        store(m, 2049, 3073)
         scale_on_vector(m, 3072, 4096)
-        store(m, 0, 4097)
+        store(m, 3073, 4097)

from contextlib import ExitStack

import concourse.mybir as mybir
from concourse.masks import make_identity

FLOPS = 2 * 1024 * 4096 * 1024

F32 = mybir.dt.float32
BF16 = mybir.dt.bfloat16
U32 = mybir.dt.uint32
U8 = mybir.dt.uint8
I32 = mybir.dt.int32
FP8X4 = mybir.dt.float8_e4m3fn_x4
ALU = mybir.AluOpType
ACT = mybir.ActivationFunctionType
AX = mybir.AxisListType

P = 128
NT = 8
NCH = 8
PAD = 32
XP = PAD + 1024
WP = XP // 2
OPAD = 8
WBUFS = 4
X_LAG = 2


def tile_lorentzmlp_pa_kernel(tc, x_hyp, W, b, out):
    nc = tc.nc
    with ExitStack() as ctx:
        ctx.enter_context(tc.manual_schedule())
        const = ctx.enter_context(tc.tile_pool(name="const", bufs=1))
        wpool = ctx.enter_context(tc.tile_pool(name="wraw", bufs=WBUFS))
        gpool = ctx.enter_context(tc.tile_pool(name="grouped", bufs=2))
        tpool = ctx.enter_context(tc.tile_pool(name="ts", bufs=4))
        spool = ctx.enter_context(tc.tile_pool(name="scratch", bufs=2))
        opool = ctx.enter_context(tc.tile_pool(name="outs", bufs=4))
        small = ctx.enter_context(tc.tile_pool(name="small", bufs=3))
        psum = ctx.enter_context(tc.psum_pool(name="psum", bufs=8))

        xraw = const.tile([P, NT * XP], BF16, align_bytes=64)
        xr3 = xraw[:].rearrange("p (m c) -> p m c", c=XP)
        xsrc = x_hyp.rearrange("(m p) c -> p m c", p=P)
        wsrc = W[1:4097, :].rearrange("(c t p) k -> c p t k", t=4, p=P)
        xq = const.tile([P, NT * 256], U32, align_bytes=64)
        xsc = const.tile([P, NT * 256], U8, align_bytes=64)
        wq = const.tile([P, NCH * 1024], U32, align_bytes=64)
        wsc = const.tile([P, NCH * 1024], U8, align_bytes=64)
        bias = const.tile([P, 4096], BF16)
        brow = const.tile([P, 4096], BF16)
        ones = const.tile([P, P], BF16)
        ident_f = const.tile([P, P], F32)
        ident_b = const.tile([P, P], BF16)
        one = const.tile([P, 1], F32)
        ex2 = const.tile([P, 2], F32)
        warm = const.tile([P, 2], F32)
        pw = const.tile([P, 16], F32)
        pw3 = pw[:].rearrange("p (a i) -> p a i", i=8)
        pc = const.tile([P, 16], F32)
        v = const.tile([P, 8], F32)
        v3 = v[:].rearrange("p (a i) -> p a i", a=2)
        vp1 = const.tile([P, 8], F32)
        po = const.tile([P, 16], F32)
        rns = const.tile([P, 8], F32)
        warg = const.tile([P, 8], F32)
        dist = const.tile([P, 8], F32)
        sx = const.tile([P, 8], F32)

        wraw_t = {}
        wbank = {}
        wg_t = {}
        ts_t = {}
        xbank = {}
        xg_t = {}
        bbank = {}

        def load_w(c):
            wraw = wpool.tile([P, 4 * XP], BF16, align_bytes=64, name="wraw")
            nc.sync.dma_start(
                out=wraw[:].rearrange("p (t k) -> p t k", k=XP)[:, :, PAD - 1 : XP],
                in_=wsrc[c],
            )
            wraw_t[c] = wraw

        def row_norm(m):
            xs = xr3[:, m, PAD:XP]
            if m % 2 == 0:
                junk = spool.tile([P, 1024], BF16, name="junk")
                nc.scalar.activation(
                    out=junk[:], in_=xs, func=ACT.Square,
                    accum_out=pw3[:, 0, m // 2 : m // 2 + 1],
                )
            else:
                junkv = spool.tile([P, 1024], F32, name="junkv")
                nc.vector.scalar_tensor_tensor(
                    out=junkv[:], in0=xs, scalar=1.0, in1=xs,
                    op0=ALU.mult, op1=ALU.mult,
                    accum_out=pw3[:, 1, m // 2 : m // 2 + 1],
                )

        def scale_x(m):
            j = 4 * (m % 2) + m // 2
            ts = tpool.tile([P, 1024], BF16, align_bytes=64, name="ts")
            nc.vector.tensor_scalar(
                out=ts[:], in0=xr3[:, m, PAD:XP], scalar1=sx[:, j : j + 1],
                scalar2=None, op0=ALU.mult,
            )
            ts_t[m] = ts

        def transpose_x(m):
            xt = psum.tile([P, 1024], BF16, tag="bank", name="xt")
            ts3 = ts_t[m][:].rearrange("p (q e) -> p e q", e=2)
            for g in range(2):
                for u in range(2):
                    for e in range(2):
                        col = (g * 4 + 2 * u + e) * P
                        src = 256 * g + 128 * u
                        nc.tensor.transpose(
                            xt[:, col : col + P], ts3[:, e, src : src + P], ident_b[:]
                        )
            xbank[m] = xt

        def regroup_x(m):
            xg = gpool.tile([P, 1024], BF16, align_bytes=64, name="xg")
            dst = xg[:].rearrange("p (g r t) -> p g r t", g=2, t=4)
            src = xbank[m][:].rearrange("p (g t r) -> p g r t", g=2, t=4)
            if m % 2 == 1 and m >= NT // 2:
                nc.scalar.copy(out=dst, in_=src)
            else:
                nc.vector.tensor_copy(out=dst, in_=src)
            xg_t[m] = xg

        def quantise_x(m):
            nc.vector.quantize_mx(
                out=xq[:, m * 256 : (m + 1) * 256].bitcast(FP8X4),
                scales=xsc[:, m * 256 : (m + 1) * 256],
                in_=xg_t[m][:],
            )

        def transpose_w(c):
            wf = wraw_t[c][:].bitcast(F32)
            for g in range(2):
                for tp in range(2):
                    wt = psum.tile([P, 512], F32, tag="bank", name="wt")
                    for tl in range(2):
                        for u in range(2):
                            col = (tl * 2 + u) * P
                            src = (2 * tp + tl) * WP + PAD // 2 + 256 * g + 128 * u
                            nc.tensor.transpose(
                                wt[:, col : col + P], wf[:, src : src + P], ident_f[:]
                            )
                    wbank[(c, 2 * g + tp)] = wt

        def copy_w(c, k, on_vector):
            if c not in wg_t:
                wg = gpool.tile([P, 4096], BF16, align_bytes=64, name="wg")
                wg_t[c] = wg
            wgf = wg_t[c][:].bitcast(F32)
            dst = wgf[:, k * 512 : (k + 1) * 512].rearrange(
                "p (tl n u) -> p tl n u", tl=2, u=2
            )
            src = wbank[(c, k)][:].rearrange("p (tl u n) -> p tl n u", tl=2, u=2)
            if on_vector:
                nc.vector.tensor_copy(out=dst, in_=src)
            else:
                nc.scalar.copy(out=dst, in_=src)

        def spread_bias(c):
            bp = psum.tile([P, 512], F32, tag="bank", name="bp")
            nc.tensor.matmul(
                out=bp[:], lhsT=ones[:], rhs=brow[:, 512 * c : 512 * (c + 1)],
                start=True, stop=True,
            )
            bbank[c] = bp

        def copy_bias(c):
            dst = bias[:, 512 * c : 512 * (c + 1)]
            if c % 2 == 1:
                nc.scalar.copy(out=dst, in_=bbank[c][:])
            else:
                nc.vector.tensor_copy(out=dst, in_=bbank[c][:])

        def quantise_w(c):
            nc.vector.quantize_mx(
                out=wq[:, c * 1024 : (c + 1) * 1024].bitcast(FP8X4),
                scales=wsc[:, c * 1024 : (c + 1) * 1024],
                in_=wg_t[c][:],
            )

        nc.vector.memset(brow[:].bitcast(I32), 0)
        nc.scalar.dma_start(out=brow[0:1, :], in_=b[1:4097].unsqueeze(0))
        nc.vector.memset(ones[:], 1.0)
        for h in range(4):
            nc.sync.dma_start(
                out=xr3[:, 2 * h : 2 * h + 2, PAD - 1 : XP],
                in_=xsrc[:, 2 * h : 2 * h + 2, :],
            )
        for c in range(WBUFS):
            load_w(c)
        make_identity(nc, ident_f[:])
        make_identity(nc, ident_b[:])
        nc.vector.memset(one[:], 1.0)
        nc.vector.memset(ex2[:, 0:1], 0.5)
        nc.vector.memset(ex2[:, 1:2], -0.5)
        nc.scalar.activation(out=warm[:, 0:1], in_=one[:], func=ACT.Sqrt)
        for m in range(NT - 1):
            row_norm(m)
        nc.vector.tensor_scalar_max(
            out=v3, in0=xr3[:, :, PAD - 1].rearrange("p (i a) -> p a i", a=2),
            scalar1=1.0 + 1e-7,
        )
        nc.vector.tensor_scalar_add(out=vp1[:], in0=v[:], scalar1=1.0)
        nc.vector.scalar_tensor_tensor(
            out=pc[:, 8:16], in0=v[:], scalar=-1.0, in1=vp1[:],
            op0=ALU.add, op1=ALU.mult,
        )
        row_norm(NT - 1)
        nc.vector.tensor_scalar_max(
            out=pc[:, 0:8].rearrange("p (a i) -> p a i", a=2), in0=pw3[:, :, 0:4],
            scalar1=1e-14,
        )
        nc.scalar.activation(out=po[:], in_=pc[:], func=ACT.Sqrt)
        nc.vector.tensor_tensor(out=warg[:], in0=v[:], in1=po[:, 8:16], op=ALU.add)
        nc.vector.reciprocal(out=rns[:], in_=po[:, 0:8])
        nc.scalar.activation(out=dist[:], in_=warg[:], func=ACT.Ln)
        nc.vector.tensor_tensor(out=sx[:], in0=rns[:], in1=dist[:], op=ALU.mult)

        for c in range(NCH + X_LAG):
            if c < NCH:
                transpose_w(c)
            if 1 <= c <= NT:
                transpose_x(c - 1)
            if c + WBUFS < NCH:
                load_w(c + WBUFS)
            if c < NCH:
                spread_bias(c)
            if c == 0:
                scale_x(0)
                scale_x(1)
            if c < NCH:
                for k in range(4):
                    copy_w(c, k, False)
                copy_bias(c)
            m = c - X_LAG
            if c == NCH:
                quantise_w(c - 1)
            if 0 <= m:
                regroup_x(m)
            if 1 <= c < NCH:
                quantise_w(c - 1)
            if c + 2 < NT:
                scale_x(c + 2)
            if 0 <= m and not (m % 2 == 1 and m >= NT // 2):
                quantise_x(m)
            if m % 2 == 0 and m - 1 >= NT // 2:
                quantise_x(m - 1)
        nc.scalar.activation(out=warm[:, 1:2], in_=one[:], func=ACT.Exp)

        ot_t = {}
        acc_t = {}
        n2_t = {}
        nr_t = {}
        ncl_t = {}
        ep_t = {}
        em_t = {}
        sc_t = {}

        def columns(m, lo, hi):
            return ot_t[m][:, OPAD + lo : OPAD + hi]

        def scale_on_gpsimd(m, lo, hi):
            seg = columns(m, lo, hi)
            nc.gpsimd.tensor_scalar(
                out=seg, in0=seg, scalar1=sc_t[m][:, 0:1], scalar2=0.0,
                op0=ALU.mult, op1=ALU.add,
            )

        def scale_on_vector(m, lo, hi):
            seg = columns(m, lo, hi)
            nc.vector.tensor_scalar(
                out=seg, in0=seg, scalar1=sc_t[m][:, 0:1], scalar2=None, op0=ALU.mult
            )

        def scale_on_scalar(m, lo, hi):
            seg = columns(m, lo, hi)
            nc.scalar.activation(out=seg, in_=seg, func=ACT.Copy, scale=sc_t[m][:, 0:1])

        def store(m, lo, hi):
            nc.sync.dma_start(
                out=out[m * P : (m + 1) * P, lo:hi],
                in_=ot_t[m][:, OPAD - 1 + lo : OPAD - 1 + hi],
            )

        def norm_sum(m):
            n2 = small.tile([P, 1], F32, name="n2")
            junk8 = small.tile([P, 8], F32, name="junk8")
            width = acc_t[m][:].shape[1]
            nc.scalar.activation(
                out=junk8[:, 0:width], in_=acc_t[m][:], func=ACT.Copy, accum_out=n2[:]
            )
            n2_t[m] = n2

        def norm_root(m):
            pr = small.tile([P, 2], F32, name="pr")
            nc.gpsimd.tensor_scalar(
                out=pr[:], in0=n2_t[m][:].to_broadcast([P, 2]), scalar1=1e-14,
                scalar2=None, op0=ALU.max,
            )
            nr = small.tile([P, 2], F32, name="nr")
            nc.gpsimd.tensor_tensor(out=nr[:], in0=pr[:], in1=ex2[:], op=ALU.pow)
            ncl = small.tile([P, 1], F32, name="ncl")
            nc.gpsimd.tensor_scalar(
                out=ncl[:], in0=nr[:, 0:1], scalar1=10.0, scalar2=None, op0=ALU.min
            )
            nr_t[m] = nr
            ncl_t[m] = ncl

        def norm_exp(m):
            ep = small.tile([P, 1], F32, name="ep")
            nc.scalar.activation(out=ep[:], in_=ncl_t[m][:], func=ACT.Exp)
            em = small.tile([P, 1], F32, name="em")
            nc.scalar.activation(out=em[:], in_=ncl_t[m][:], func=ACT.Exp, scale=-1.0)
            ep_t[m] = ep
            em_t[m] = em

        def norm_end(m):
            sh = small.tile([P, 1], F32, name="sh")
            nc.vector.tensor_scalar(
                out=sh[:], in0=ep_t[m][:], scalar1=em_t[m][:, 0:1], scalar2=0.5,
                op0=ALU.subtract, op1=ALU.mult,
            )
            sc = small.tile([P, 1], F32, name="sc")
            nc.vector.tensor_scalar(
                out=sc[:], in0=sh[:], scalar1=nr_t[m][:, 1:2], scalar2=None, op0=ALU.mult
            )
            nc.vector.tensor_scalar(
                out=ot_t[m][:, OPAD - 1 : OPAD], in0=ep_t[m][:],
                scalar1=em_t[m][:, 0:1], scalar2=0.5, op0=ALU.add, op1=ALU.mult,
            )
            sc_t[m] = sc

        for m in range(NT):
            last = m == NT - 1
            hw = 1 if last else 2
            ot = opool.tile([P, OPAD + 4096], F32, name="ot")
            ot_t[m] = ot
            acc = small.tile([P, NCH // hw], F32, name="acc8" if last else "acc")
            acc_t[m] = acc
            for c in range(NCH):
                ps = psum.tile([P, 512], F32, tag="bank", name="ps")
                for g in range(2):
                    lo = (2 * m + g) * P
                    ro = c * 1024 + g * 512
                    nc.tensor.matmul_mx(
                        out=ps[:],
                        lhsT=xq[:, lo : lo + P].bitcast(FP8X4),
                        lhsT_scale=xsc[:, lo : lo + P],
                        rhs=wq[:, ro : ro + 512].bitcast(FP8X4),
                        rhs_scale=wsc[:, ro : ro + 512],
                        start=(g == 0),
                        stop=(g == 1),
                    )
                nc.vector.tensor_tensor(
                    out=ot[:, OPAD + 512 * c : OPAD + 512 * (c + 1)], in0=ps[:],
                    in1=bias[:, 512 * c : 512 * (c + 1)], op=ALU.add,
                )
                if (c + 1) % hw == 0:
                    h = c // hw
                    junk = spool.tile([P, 1024], BF16, name="junk")
                    nc.scalar.activation(
                        out=junk[:, 0 : 512 * hw],
                        in_=ot[:, OPAD + 512 * hw * h : OPAD + 512 * hw * (h + 1)],
                        func=ACT.Square, accum_out=acc[:, h : h + 1],
                    )
                if m == 0 and c == 3:
                    quantise_x(NT - 1)
                if m > 0 and c == 1:
                    norm_root(m - 1)
                    if m > 1:
                        scale_on_gpsimd(m - 2, 3072, 4096)
                        store(m - 2, 2049, 4097)
                if m > 0 and c == 3:
                    norm_exp(m - 1)
                if c == NCH - 1:
                    norm_sum(m)
                    if m > 0:
                        norm_end(m - 1)
                        scale_on_vector(m - 1, 0, 1536)
                        if not last:
                            scale_on_gpsimd(m - 1, 1536, 2048)
                            store(m - 1, 0, 2049)
                            scale_on_gpsimd(m - 1, 2048, 3072)

        m = NT - 1
        norm_root(m)
        scale_on_vector(m - 1, 1536, 2048)
        store(m - 1, 0, 2049)
        scale_on_scalar(m - 1, 2048, 3072)
        scale_on_vector(m - 1, 3072, 4096)
        store(m - 1, 2049, 4097)
        norm_exp(m)
        norm_end(m)
        scale_on_vector(m, 0, 1024)
        store(m, 0, 1025)
        scale_on_gpsimd(m, 1024, 2048)
        store(m, 1025, 2049)
        scale_on_scalar(m, 2048, 3072)
        store(m, 2049, 3073)
        scale_on_vector(m, 3072, 4096)
        store(m, 3073, 4097)
